import numpy as np
import ml_dtypes


def mxq(x, axis, fmt="e4m3"):
    dtype, down = {"e4m3": (ml_dtypes.float8_e4m3fn, 7), "e5m2": (ml_dtypes.float8_e5m2, 14)}[fmt]
    v = np.moveaxis(np.asarray(x, np.float32).astype(ml_dtypes.bfloat16).astype(np.float64), axis, -1)
    blocks = v.reshape(v.shape[:-1] + (-1, 32))
    amax = np.abs(blocks).max(-1, keepdims=True)
    byte = np.maximum(np.where(amax > 0, np.frexp(amax)[1] - 1 + 127, 0) - down, 1)
    scale = np.exp2(byte - 127.0)
    codes = (blocks / scale).astype(np.float32).astype(dtype).astype(np.float64)
    return np.moveaxis((codes * scale).reshape(v.shape), -1, axis)


WIDE = False


def mx_kscale(k):
    if not WIDE:
        return np.ones(k)
    levels = np.array([20, -20, 10, -10, 0])
    a = np.random.permutation(np.resize(levels, k // 512 * 4)).reshape(k // 512, 4)
    idx = np.arange(k)
    return np.exp2(a[idx // 512, idx % 128 // 32])


BF16 = ml_dtypes.bfloat16


def bf(x):
    return np.asarray(x, np.float32).astype(BF16)


def f64(x):
    return np.asarray(x).astype(np.float64)


N, C, O, TH, TW = 2, 512, 512, 32, 64
T = N * TH * TW
BN_EPS = 1e-5
IMG_SIZES = [(max(TH >> (l + 1), 1), max(TW >> (l + 1), 1)) for l in range(5)]


def setup_inputs():
    s = mx_kscale(T).reshape(N, 1, TH, TW)
    inp = {}
    for l, (h, w) in enumerate(IMG_SIZES):
        inp[f'img_feat{l}'] = bf(np.random.standard_normal((N, C, h, w)) * 0.5)
    x0 = bf(np.random.standard_normal((N, C, TH, TW)))
    inp['pts_feat0'] = bf(f64(x0) * s)
    inp['img_w'] = bf(np.random.standard_normal((O, C)) / np.sqrt(C))
    inp['img_b'] = bf(np.random.standard_normal(O) * 0.1)
    inp['img_gamma'] = bf(1.0 + 0.1 * np.random.standard_normal(O))
    inp['img_beta'] = bf(np.random.standard_normal(O) * 0.1)
    inp['img_mean'] = bf(np.random.standard_normal(O) * 0.1)
    inp['img_var'] = bf(np.random.uniform(0.5, 1.5, O))
    inp['pts_w'] = bf(np.random.standard_normal((O, C)) / np.sqrt(C))
    inp['pts_b'] = bf(np.random.standard_normal(O) * 0.1)
    inp['pts_gamma'] = bf(1.0 + 0.1 * np.random.standard_normal(O))
    inp['pts_beta'] = bf(np.random.standard_normal(O) * 0.1)
    inp['pts_mean'] = bf(np.random.standard_normal(O) * 0.1)
    inp['pts_var'] = bf(np.random.uniform(0.5, 1.5, O))
    g = bf(np.random.standard_normal((N, 2 * O, TH, TW)) * np.exp2(np.random.randint(-12, 1, (N, 1, TH, TW))) / s)
    y = (f64(inp['pts_w']) @ f64(x0).reshape(N, C, TH * TW)).reshape(N, O, TH, TW) + f64(inp['pts_b'])[None, :, None, None]
    scale = f64(inp['pts_gamma']) / np.sqrt(f64(inp['pts_var']) + BN_EPS)
    z = (y - f64(inp['pts_mean'])[None, :, None, None]) * scale[None, :, None, None] + f64(inp['pts_beta'])[None, :, None, None]
    inp['pts_z'] = np.asarray(z, np.float32)
    inp['grad_out'] = g
    return inp


def reference(img_feat0, img_feat1, img_feat2, img_feat3, img_feat4, pts_feat0,
              img_w, img_b, img_gamma, img_beta, img_mean, img_var,
              pts_w, pts_b, pts_gamma, pts_beta, pts_mean, pts_var, pts_z, grad_out):
    scale = f64(pts_gamma) / np.sqrt(f64(pts_var) + BN_EPS)
    g = f64(grad_out)[:, O:]
    dy = g * (f64(pts_z) > 0.0) * scale[None, :, None, None]
    dyt = dy.transpose(1, 0, 2, 3).reshape(O, T)
    xt = f64(pts_feat0).transpose(1, 0, 2, 3).reshape(C, T)
    return mxq(dyt, 1, "e5m2") @ mxq(xt, 1, "e4m3").T

@@ -1,0 +1,199 @@
+from contextlib import ExitStack
+
+import concourse.mybir as mybir
+from concourse.masks import make_identity
+
+F32 = mybir.dt.float32
+BF16 = mybir.dt.bfloat16
+I32 = mybir.dt.int32
+U32 = mybir.dt.uint32
+U8 = mybir.dt.uint8
+E4M3_X4 = mybir.dt.float8_e4m3fn_x4
+E5M2_X4 = mybir.dt.float8_e5m2_x4
+ALU = mybir.AluOpType
+
+P = 128
+IMAGES = 2
+CHANNELS = 512
+TOKENS = 2048
+BLOCKS = CHANNELS // P
+K_PASS = 4 * P
+PASSES = TOKENS // K_PASS
+BANK_WORDS = 512
+BANK_TOKENS = 2 * BANK_WORDS
+BANK_PASSES = BANK_TOKENS // K_PASS
+HALVES = TOKENS // BANK_TOKENS
+BN_EPS = 1e-5
+
+FLOPS = 2 * CHANNELS * CHANNELS * IMAGES * TOKENS
+BYTES = IMAGES * CHANNELS * TOKENS * (2 + 2 + 4) + 2 * CHANNELS * 2 + CHANNELS * CHANNELS * 4
+
+
+def transpose_half(nc, banks, identity, words, dest):
+    bank = banks.tile([P, BANK_WORDS], F32, name="bank")
+    for j in range(BANK_WORDS // P):
+        nc.tensor.transpose(bank[:, j * P : (j + 1) * P], words[:, j * P : (j + 1) * P], identity[:])
+    nc.scalar.copy(out=dest, in_=bank[:].rearrange("p (g u c) -> p g c u", g=BANK_PASSES, u=2))
+
+
+def tile_prefusioncat_v_kernel(
+    tc,
+    img_feat0,
+    img_feat1,
+    img_feat2,
+    img_feat3,
+    img_feat4,
+    pts_feat0,
+    img_w,
+    img_b,
+    img_gamma,
+    img_beta,
+    img_mean,
+    img_var,
+    pts_w,
+    pts_b,
+    pts_gamma,
+    pts_beta,
+    pts_mean,
+    pts_var,
+    pts_z,
+    grad_out,
+    out,
+):
+    nc = tc.nc
+    x_dram = pts_feat0.rearrange("n (b p) h w -> n b p (h w)", p=P)
+    z_dram = pts_z.rearrange("n (b p) h w -> n b p (h w)", p=P)
+    g_dram = grad_out.rearrange("n (b p) h w -> n b p (h w)", p=P)
+    out_dram = out.rearrange("(b p) c -> b p c", p=P)
+
+    with ExitStack() as ctx:
+        const = ctx.enter_context(tc.tile_pool(name="const", bufs=1))
+        raw = ctx.enter_context(tc.tile_pool(name="raw", bufs=IMAGES * BLOCKS))
+        work = ctx.enter_context(tc.tile_pool(name="work", bufs=3))
+        banks = ctx.enter_context(tc.psum_pool(name="banks", bufs=6))
+        sums = ctx.enter_context(tc.psum_pool(name="sums", bufs=2))
+
+        rows = const.tile([P, P], BF16, name="rows")
+        nc.vector.memset(rows[:].bitcast(I32), 0)
+        nc.scalar.dma_start(out=rows[0:BLOCKS, :], in_=pts_gamma.rearrange("(b p) -> b p", p=P))
+        nc.scalar.dma_start(
+            out=rows[BLOCKS : 2 * BLOCKS, :], in_=pts_var.rearrange("(b p) -> b p", p=P)
+        )
+
+        x_raw = {}
+        z_raw = {}
+        g_raw = {}
+        for n in range(IMAGES):
+            for b in range(BLOCKS):
+                x_raw[(n, b)] = raw.tile([P, TOKENS], BF16, name="x_raw")
+                nc.sync.dma_start(out=x_raw[(n, b)][:], in_=x_dram[n, b])
+        for b in range(BLOCKS):
+            for n in range(IMAGES):
+                z_raw[(n, b)] = raw.tile([P, TOKENS], F32, name="z_raw")
+                nc.sync.dma_start(out=z_raw[(n, b)][:], in_=z_dram[n, b])
+                g_raw[(n, b)] = raw.tile([P, TOKENS], BF16, name="g_raw")
+                nc.sync.dma_start(out=g_raw[(n, b)][:], in_=g_dram[n, BLOCKS + b])
+
+        identity = const.tile([P, P], F32, name="identity")
+        make_identity(nc, identity[:])
+
+        rows_f32 = const.tile([P, P], F32, name="rows_f32")
+        nc.vector.tensor_copy(out=rows_f32[:], in_=rows[:])
+        columns = banks.tile([P, BANK_WORDS], F32, name="bank")
+        nc.tensor.transpose(columns[:, 0:P], rows_f32[:], identity[:])
+        var_eps = const.tile([P, BLOCKS], F32, name="var_eps")
+        nc.vector.tensor_scalar_add(
+            out=var_eps[:], in0=columns[:, BLOCKS : 2 * BLOCKS], scalar1=BN_EPS
+        )
+        std = const.tile([P, BLOCKS], F32, name="std")
+        nc.scalar.sqrt(out=std[:], in_=var_eps[:])
+        inv_std = const.tile([P, BLOCKS], F32, name="inv_std")
+        nc.vector.reciprocal(out=inv_std[:], in_=std[:])
+        scale = const.tile([P, BLOCKS], F32, name="scale")
+        nc.vector.tensor_mul(out=scale[:], in0=columns[:, 0:BLOCKS], in1=inv_std[:])
+
+        x_codes = const.tile([P, IMAGES * PASSES, CHANNELS], U32, name="x_codes", align_bytes=64)
+        x_scales = const.tile([P, IMAGES * PASSES, CHANNELS], U8, name="x_scales", align_bytes=64)
+        for n in range(IMAGES):
+            x_grouped = const.tile(
+                [P, PASSES * CHANNELS * 4], BF16, name="x_grouped%d" % n, align_bytes=64
+            )
+            x_grouped_words = x_grouped[:].bitcast(F32).rearrange(
+                "p (g c u) -> p g c u", g=PASSES, u=2
+            )
+            for b in range(BLOCKS):
+                for half in range(HALVES):
+                    transpose_half(
+                        nc,
+                        banks,
+                        identity,
+                        x_raw[(n, b)][:].bitcast(F32)[:, half * BANK_WORDS : (half + 1) * BANK_WORDS],
+                        x_grouped_words[
+                            :, half * BANK_PASSES : (half + 1) * BANK_PASSES, b * P : (b + 1) * P, :
+                        ],
+                    )
+            for g in range(PASSES):
+                nc.vector.quantize_mx(
+                    out=x_codes[:, n * PASSES + g, :].bitcast(E4M3_X4),
+                    scales=x_scales[:, n * PASSES + g, :],
+                    in_=x_grouped[:, g * CHANNELS * 4 : (g + 1) * CHANNELS * 4],
+                )
+
+        def form_dy(n, b, half):
+            cols = slice(half * BANK_TOKENS, (half + 1) * BANK_TOKENS)
+            mask = work.tile([P, BANK_TOKENS], BF16, name="mask")
+            nc.vector.tensor_scalar(
+                out=mask[:], in0=z_raw[(n, b)][:, cols], scalar1=0.0, scalar2=None, op0=ALU.is_gt
+            )
+            scaled = work.tile([P, BANK_TOKENS], BF16, name="scaled")
+            nc.vector.tensor_scalar(
+                out=scaled[:],
+                in0=g_raw[(n, b)][:, cols],
+                scalar1=scale[:, b : b + 1],
+                scalar2=None,
+                op0=ALU.mult,
+            )
+            dy = work.tile([P, BANK_TOKENS], BF16, name="dy")
+            nc.vector.tensor_mul(out=dy[:], in0=scaled[:], in1=mask[:])
+            dy_grouped = work.tile([P, BANK_TOKENS], BF16, name="dy_grouped", align_bytes=64)
+            transpose_half(
+                nc,
+                banks,
+                identity,
+                dy[:].bitcast(F32),
+                dy_grouped[:].bitcast(F32).rearrange("p (g c u) -> p g c u", g=BANK_PASSES, u=2),
+            )
+            return dy_grouped
+
+        def multiply(n, b, half, dy_grouped, acc):
+            dy_codes = work.tile([P, BANK_PASSES * P], U32, name="dy_codes", align_bytes=64)
+            dy_scales = work.tile([P, BANK_PASSES * P], U8, name="dy_scales", align_bytes=64)
+            nc.vector.quantize_mx(
+                out=dy_codes[:].bitcast(E5M2_X4), scales=dy_scales[:], in_=dy_grouped[:]
+            )
+            for j in range(BANK_PASSES):
+                g = n * PASSES + half * BANK_PASSES + j
+                nc.tensor.matmul_mx(
+                    out=acc[:],
+                    lhsT=dy_codes[:, j * P : (j + 1) * P].bitcast(E5M2_X4),
+                    lhsT_scale=dy_scales[:, j * P : (j + 1) * P],
+                    rhs=x_codes[:, g, :].bitcast(E4M3_X4),
+                    rhs_scale=x_scales[:, g, :],
+                    start=(g == 0),
+                    stop=(g == IMAGES * PASSES - 1),
+                )
+            if n == IMAGES - 1 and half == HALVES - 1:
+                result = work.tile([P, CHANNELS], F32, name="result")
+                nc.scalar.copy(out=result[:], in_=acc[:])
+                nc.sync.dma_start(out=out_dram[b], in_=result[:])
+
+        waiting = None
+        for b in range(BLOCKS):
+            acc = sums.tile([P, CHANNELS], F32, name="acc")
+            for n in range(IMAGES):
+                for half in range(HALVES):
+                    formed = (n, b, half, form_dy(n, b, half), acc)
+                    if waiting is not None:
+                        multiply(*waiting)
+                    waiting = formed
+        multiply(*waiting)

@@ -5,7 +5,6 @@ from concourse.masks import make_identity
 
 F32 = mybir.dt.float32
 BF16 = mybir.dt.bfloat16
-I32 = mybir.dt.int32
 U32 = mybir.dt.uint32
 U8 = mybir.dt.uint8
 E4M3_X4 = mybir.dt.float8_e4m3fn_x4
@@ -16,24 +15,17 @@ P = 128
 IMAGES = 2
 CHANNELS = 512
 TOKENS = 2048
-BLOCKS = CHANNELS // P
+TILES = CHANNELS // P
 K_PASS = 4 * P
 PASSES = TOKENS // K_PASS
 BANK_WORDS = 512
-BANK_TOKENS = 2 * BANK_WORDS
-BANK_PASSES = BANK_TOKENS // K_PASS
-HALVES = TOKENS // BANK_TOKENS
+HALF_TOKENS = 2 * BANK_WORDS
+HALF_PASSES = HALF_TOKENS // K_PASS
+HALVES = TOKENS // HALF_TOKENS
 BN_EPS = 1e-5
 
 FLOPS = 2 * CHANNELS * CHANNELS * IMAGES * TOKENS
 BYTES = IMAGES * CHANNELS * TOKENS * (2 + 2 + 4) + 2 * CHANNELS * 2 + CHANNELS * CHANNELS * 4
-
-
-def transpose_half(nc, banks, identity, words, dest):
-    bank = banks.tile([P, BANK_WORDS], F32, name="bank")
-    for j in range(BANK_WORDS // P):
-        nc.tensor.transpose(bank[:, j * P : (j + 1) * P], words[:, j * P : (j + 1) * P], identity[:])
-    nc.scalar.copy(out=dest, in_=bank[:].rearrange("p (g u c) -> p g c u", g=BANK_PASSES, u=2))
 
 
 def tile_prefusioncat_v_kernel(
@@ -61,139 +53,138 @@ def tile_prefusioncat_v_kernel(
     out,
 ):
     nc = tc.nc
-    x_dram = pts_feat0.rearrange("n (b p) h w -> n b p (h w)", p=P)
-    z_dram = pts_z.rearrange("n (b p) h w -> n b p (h w)", p=P)
-    g_dram = grad_out.rearrange("n (b p) h w -> n b p (h w)", p=P)
-    out_dram = out.rearrange("(b p) c -> b p c", p=P)
+    x_dram = pts_feat0.rearrange("n (j p) h w -> n j p (h w)", p=P)
+    z_dram = pts_z.rearrange("n (p j) h w -> n j p (h w)", j=TILES)
+    g_dram = grad_out.rearrange("n (s p j) h w -> n s j p (h w)", s=2, j=TILES)
+    out_dram = out.rearrange("(p j) c -> j p c", j=TILES)
 
     with ExitStack() as ctx:
+        ctx.enter_context(tc.manual_schedule())
         const = ctx.enter_context(tc.tile_pool(name="const", bufs=1))
-        raw = ctx.enter_context(tc.tile_pool(name="raw", bufs=IMAGES * BLOCKS))
-        work = ctx.enter_context(tc.tile_pool(name="work", bufs=3))
-        banks = ctx.enter_context(tc.psum_pool(name="banks", bufs=6))
-        sums = ctx.enter_context(tc.psum_pool(name="sums", bufs=2))
+        raw = ctx.enter_context(tc.tile_pool(name="raw", bufs=IMAGES * TILES))
+        work = ctx.enter_context(tc.tile_pool(name="work", bufs=4))
+        banks = ctx.enter_context(tc.psum_pool(name="banks", bufs=4))
+        sums = ctx.enter_context(tc.psum_pool(name="sums", bufs=1))
 
-        rows = const.tile([P, P], BF16, name="rows")
-        nc.vector.memset(rows[:].bitcast(I32), 0)
-        nc.scalar.dma_start(out=rows[0:BLOCKS, :], in_=pts_gamma.rearrange("(b p) -> b p", p=P))
-        nc.scalar.dma_start(
-            out=rows[BLOCKS : 2 * BLOCKS, :], in_=pts_var.rearrange("(b p) -> b p", p=P)
-        )
+        var = const.tile([P, TILES], BF16, name="var")
+        nc.sync.dma_start(out=var[:], in_=pts_var.rearrange("(p j) -> p j", j=TILES))
+        gamma = const.tile([P, TILES], BF16, name="gamma")
+        nc.sync.dma_start(out=gamma[:], in_=pts_gamma.rearrange("(p j) -> p j", j=TILES))
 
         x_raw = {}
         z_raw = {}
         g_raw = {}
-        for n in range(IMAGES):
-            for b in range(BLOCKS):
-                x_raw[(n, b)] = raw.tile([P, TOKENS], BF16, name="x_raw")
-                nc.sync.dma_start(out=x_raw[(n, b)][:], in_=x_dram[n, b])
-        for b in range(BLOCKS):
-            for n in range(IMAGES):
-                z_raw[(n, b)] = raw.tile([P, TOKENS], F32, name="z_raw")
-                nc.sync.dma_start(out=z_raw[(n, b)][:], in_=z_dram[n, b])
-                g_raw[(n, b)] = raw.tile([P, TOKENS], BF16, name="g_raw")
-                nc.sync.dma_start(out=g_raw[(n, b)][:], in_=g_dram[n, BLOCKS + b])
+        halves = []
+
+        def load_x(n, j):
+            x_raw[(n, j)] = raw.tile([P, TOKENS], BF16, name="x_raw")
+            nc.sync.dma_start(out=x_raw[(n, j)][:], in_=x_dram[n, j])
+            halves.extend([("x", n, j, half) for half in range(HALVES)])
+
+        def load_dy_inputs(n, j):
+            z_raw[(n, j)] = raw.tile([P, TOKENS], F32, name="z_raw")
+            nc.sync.dma_start(out=z_raw[(n, j)][:], in_=z_dram[n, j])
+            g_raw[(n, j)] = raw.tile([P, TOKENS], BF16, name="g_raw")
+            nc.sync.dma_start(out=g_raw[(n, j)][:], in_=g_dram[n, 1, j])
+            halves.extend([("dy", n, j, half) for half in range(HALVES)])
+
+        for j in range(TILES):
+            load_x(0, j)
+        for j in range(TILES):
+            load_dy_inputs(0, j)
+            load_x(1, j)
+        for j in range(TILES):
+            load_dy_inputs(1, j)
 
         identity = const.tile([P, P], F32, name="identity")
         make_identity(nc, identity[:])
 
-        rows_f32 = const.tile([P, P], F32, name="rows_f32")
-        nc.vector.tensor_copy(out=rows_f32[:], in_=rows[:])
-        columns = banks.tile([P, BANK_WORDS], F32, name="bank")
-        nc.tensor.transpose(columns[:, 0:P], rows_f32[:], identity[:])
-        var_eps = const.tile([P, BLOCKS], F32, name="var_eps")
-        nc.vector.tensor_scalar_add(
-            out=var_eps[:], in0=columns[:, BLOCKS : 2 * BLOCKS], scalar1=BN_EPS
-        )
-        std = const.tile([P, BLOCKS], F32, name="std")
+        var_eps = const.tile([P, TILES], F32, name="var_eps")
+        nc.vector.tensor_scalar_add(out=var_eps[:], in0=var[:], scalar1=BN_EPS)
+        std = const.tile([P, TILES], F32, name="std")
         nc.scalar.sqrt(out=std[:], in_=var_eps[:])
-        inv_std = const.tile([P, BLOCKS], F32, name="inv_std")
+        inv_std = const.tile([P, TILES], F32, name="inv_std")
         nc.vector.reciprocal(out=inv_std[:], in_=std[:])
-        scale = const.tile([P, BLOCKS], F32, name="scale")
-        nc.vector.tensor_mul(out=scale[:], in0=columns[:, 0:BLOCKS], in1=inv_std[:])
+        scale = const.tile([P, TILES], F32, name="scale")
+        nc.vector.tensor_mul(out=scale[:], in0=gamma[:], in1=inv_std[:])
 
         x_codes = const.tile([P, IMAGES * PASSES, CHANNELS], U32, name="x_codes", align_bytes=64)
         x_scales = const.tile([P, IMAGES * PASSES, CHANNELS], U8, name="x_scales", align_bytes=64)
-        for n in range(IMAGES):
-            x_grouped = const.tile(
-                [P, PASSES * CHANNELS * 4], BF16, name="x_grouped%d" % n, align_bytes=64
-            )
-            x_grouped_words = x_grouped[:].bitcast(F32).rearrange(
-                "p (g c u) -> p g c u", g=PASSES, u=2
-            )
-            for b in range(BLOCKS):
-                for half in range(HALVES):
-                    transpose_half(
-                        nc,
-                        banks,
-                        identity,
-                        x_raw[(n, b)][:].bitcast(F32)[:, half * BANK_WORDS : (half + 1) * BANK_WORDS],
-                        x_grouped_words[
-                            :, half * BANK_PASSES : (half + 1) * BANK_PASSES, b * P : (b + 1) * P, :
-                        ],
-                    )
-            for g in range(PASSES):
-                nc.vector.quantize_mx(
-                    out=x_codes[:, n * PASSES + g, :].bitcast(E4M3_X4),
-                    scales=x_scales[:, n * PASSES + g, :],
-                    in_=x_grouped[:, g * CHANNELS * 4 : (g + 1) * CHANNELS * 4],
-                )
+        acc = [sums.tile([P, CHANNELS], F32, name="acc%d" % j) for j in range(TILES)]
 
-        def form_dy(n, b, half):
-            cols = slice(half * BANK_TOKENS, (half + 1) * BANK_TOKENS)
-            mask = work.tile([P, BANK_TOKENS], BF16, name="mask")
+        def form_dy(n, j, half):
+            cols = slice(half * HALF_TOKENS, (half + 1) * HALF_TOKENS)
+            mask = work.tile([P, HALF_TOKENS], BF16, name="mask")
             nc.vector.tensor_scalar(
-                out=mask[:], in0=z_raw[(n, b)][:, cols], scalar1=0.0, scalar2=None, op0=ALU.is_gt
+                out=mask[:], in0=z_raw[(n, j)][:, cols], scalar1=0.0, scalar2=None, op0=ALU.is_gt
             )
-            scaled = work.tile([P, BANK_TOKENS], BF16, name="scaled")
+            scaled = work.tile([P, HALF_TOKENS], BF16, name="scaled")
             nc.vector.tensor_scalar(
                 out=scaled[:],
-                in0=g_raw[(n, b)][:, cols],
-                scalar1=scale[:, b : b + 1],
+                in0=g_raw[(n, j)][:, cols],
+                scalar1=scale[:, j : j + 1],
                 scalar2=None,
                 op0=ALU.mult,
             )
-            dy = work.tile([P, BANK_TOKENS], BF16, name="dy")
+            dy = work.tile([P, HALF_TOKENS], BF16, name="dy")
             nc.vector.tensor_mul(out=dy[:], in0=scaled[:], in1=mask[:])
-            dy_grouped = work.tile([P, BANK_TOKENS], BF16, name="dy_grouped", align_bytes=64)
-            transpose_half(
-                nc,
-                banks,
-                identity,
-                dy[:].bitcast(F32),
-                dy_grouped[:].bitcast(F32).rearrange("p (g c u) -> p g c u", g=BANK_PASSES, u=2),
-            )
-            return dy_grouped
+            return dy
 
-        def multiply(n, b, half, dy_grouped, acc):
-            dy_codes = work.tile([P, BANK_PASSES * P], U32, name="dy_codes", align_bytes=64)
-            dy_scales = work.tile([P, BANK_PASSES * P], U8, name="dy_scales", align_bytes=64)
-            nc.vector.quantize_mx(
-                out=dy_codes[:].bitcast(E5M2_X4), scales=dy_scales[:], in_=dy_grouped[:]
+        def begin(operand, n, j, half):
+            if operand == "x":
+                words = x_raw[(n, j)][:].bitcast(F32)[:, half * BANK_WORDS : (half + 1) * BANK_WORDS]
+            else:
+                words = form_dy(n, j, half)[:].bitcast(F32)
+            bank = banks.tile([P, BANK_WORDS], F32, name="bank")
+            for s in range(BANK_WORDS // P):
+                nc.tensor.transpose(
+                    bank[:, s * P : (s + 1) * P], words[:, s * P : (s + 1) * P], identity[:]
+                )
+            grouped = work.tile([P, HALF_TOKENS], BF16, name="grouped", align_bytes=64)
+            nc.scalar.copy(
+                out=grouped[:].bitcast(F32).rearrange("p (g c u) -> p g c u", g=HALF_PASSES, u=2),
+                in_=bank[:].rearrange("p (g u c) -> p g c u", g=HALF_PASSES, u=2),
             )
-            for j in range(BANK_PASSES):
-                g = n * PASSES + half * BANK_PASSES + j
+            return grouped
+
+        def finish_x(n, j, half, grouped):
+            for g in range(HALF_PASSES):
+                k = n * PASSES + half * HALF_PASSES + g
+                nc.vector.quantize_mx(
+                    out=x_codes[:, k, j * P : (j + 1) * P].bitcast(E4M3_X4),
+                    scales=x_scales[:, k, j * P : (j + 1) * P],
+                    in_=grouped[:, g * 4 * P : (g + 1) * 4 * P],
+                )
+
+        def finish_dy(n, j, half, grouped):
+            dy_codes = work.tile([P, HALF_PASSES * P], U32, name="dy_codes", align_bytes=64)
+            dy_scales = work.tile([P, HALF_PASSES * P], U8, name="dy_scales", align_bytes=64)
+            nc.vector.quantize_mx(
+                out=dy_codes[:].bitcast(E5M2_X4), scales=dy_scales[:], in_=grouped[:]
+            )
+            for g in range(HALF_PASSES):
+                k = n * PASSES + half * HALF_PASSES + g
                 nc.tensor.matmul_mx(
-                    out=acc[:],
-                    lhsT=dy_codes[:, j * P : (j + 1) * P].bitcast(E5M2_X4),
-                    lhsT_scale=dy_scales[:, j * P : (j + 1) * P],
-                    rhs=x_codes[:, g, :].bitcast(E4M3_X4),
-                    rhs_scale=x_scales[:, g, :],
-                    start=(g == 0),
-                    stop=(g == IMAGES * PASSES - 1),
+                    out=acc[j][:],
+                    lhsT=dy_codes[:, g * P : (g + 1) * P].bitcast(E5M2_X4),
+                    lhsT_scale=dy_scales[:, g * P : (g + 1) * P],
+                    rhs=x_codes[:, k, :].bitcast(E4M3_X4),
+                    rhs_scale=x_scales[:, k, :],
+                    start=(k == 0),
+                    stop=(k == IMAGES * PASSES - 1),
                 )
             if n == IMAGES - 1 and half == HALVES - 1:
                 result = work.tile([P, CHANNELS], F32, name="result")
-                nc.scalar.copy(out=result[:], in_=acc[:])
-                nc.sync.dma_start(out=out_dram[b], in_=result[:])
+                nc.scalar.copy(out=result[:], in_=acc[j][:])
+                nc.sync.dma_start(out=out_dram[j], in_=result[:])
 
-        waiting = None
-        for b in range(BLOCKS):
-            acc = sums.tile([P, CHANNELS], F32, name="acc")
-            for n in range(IMAGES):
-                for half in range(HALVES):
-                    formed = (n, b, half, form_dy(n, b, half), acc)
-                    if waiting is not None:
-                        multiply(*waiting)
-                    waiting = formed
-        multiply(*waiting)
+        grouped_of = {}
+        for i in range(len(halves) + 1):
+            if i < len(halves):
+                grouped_of[i] = begin(*halves[i])
+            if i > 0:
+                operand, n, j, half = halves[i - 1]
+                if operand == "x":
+                    finish_x(n, j, half, grouped_of[i - 1])
+                else:
+                    finish_dy(n, j, half, grouped_of[i - 1])

@@ -23,6 +23,7 @@ HALF_TOKENS = 2 * BANK_WORDS
 HALF_PASSES = HALF_TOKENS // K_PASS
 HALVES = TOKENS // HALF_TOKENS
 BN_EPS = 1e-5
+LAG = 4
 
 FLOPS = 2 * CHANNELS * CHANNELS * IMAGES * TOKENS
 BYTES = IMAGES * CHANNELS * TOKENS * (2 + 2 + 4) + 2 * CHANNELS * 2 + CHANNELS * CHANNELS * 4
@@ -62,7 +63,8 @@ def tile_prefusioncat_v_kernel(
         ctx.enter_context(tc.manual_schedule())
         const = ctx.enter_context(tc.tile_pool(name="const", bufs=1))
         raw = ctx.enter_context(tc.tile_pool(name="raw", bufs=IMAGES * TILES))
-        work = ctx.enter_context(tc.tile_pool(name="work", bufs=4))
+        work = ctx.enter_context(tc.tile_pool(name="work", bufs=3))
+        lagged = ctx.enter_context(tc.tile_pool(name="lagged", bufs=LAG + 2))
         banks = ctx.enter_context(tc.psum_pool(name="banks", bufs=4))
         sums = ctx.enter_context(tc.psum_pool(name="sums", bufs=1))
 
@@ -112,35 +114,28 @@ def tile_prefusioncat_v_kernel(
         x_scales = const.tile([P, IMAGES * PASSES, CHANNELS], U8, name="x_scales", align_bytes=64)
         acc = [sums.tile([P, CHANNELS], F32, name="acc%d" % j) for j in range(TILES)]
 
-        def form_dy(n, j, half):
-            cols = slice(half * HALF_TOKENS, (half + 1) * HALF_TOKENS)
-            mask = work.tile([P, HALF_TOKENS], BF16, name="mask")
+        def dy_factors(n, j):
+            mask = work.tile([P, TOKENS], BF16, name="mask")
             nc.vector.tensor_scalar(
-                out=mask[:], in0=z_raw[(n, j)][:, cols], scalar1=0.0, scalar2=None, op0=ALU.is_gt
+                out=mask[:], in0=z_raw[(n, j)][:], scalar1=0.0, scalar2=None, op0=ALU.is_gt
             )
-            scaled = work.tile([P, HALF_TOKENS], BF16, name="scaled")
+            scaled = work.tile([P, TOKENS], BF16, name="scaled")
             nc.vector.tensor_scalar(
                 out=scaled[:],
-                in0=g_raw[(n, j)][:, cols],
+                in0=g_raw[(n, j)][:],
                 scalar1=scale[:, j : j + 1],
                 scalar2=None,
                 op0=ALU.mult,
             )
-            dy = work.tile([P, HALF_TOKENS], BF16, name="dy")
-            nc.vector.tensor_mul(out=dy[:], in0=scaled[:], in1=mask[:])
-            return dy
+            return mask, scaled
 
-        def begin(operand, n, j, half):
-            if operand == "x":
-                words = x_raw[(n, j)][:].bitcast(F32)[:, half * BANK_WORDS : (half + 1) * BANK_WORDS]
-            else:
-                words = form_dy(n, j, half)[:].bitcast(F32)
+        def turn(words):
             bank = banks.tile([P, BANK_WORDS], F32, name="bank")
             for s in range(BANK_WORDS // P):
                 nc.tensor.transpose(
                     bank[:, s * P : (s + 1) * P], words[:, s * P : (s + 1) * P], identity[:]
                 )
-            grouped = work.tile([P, HALF_TOKENS], BF16, name="grouped", align_bytes=64)
+            grouped = lagged.tile([P, HALF_TOKENS], BF16, name="grouped", align_bytes=64)
             nc.scalar.copy(
                 out=grouped[:].bitcast(F32).rearrange("p (g c u) -> p g c u", g=HALF_PASSES, u=2),
                 in_=bank[:].rearrange("p (g u c) -> p g c u", g=HALF_PASSES, u=2),
@@ -179,12 +174,22 @@ def tile_prefusioncat_v_kernel(
                 nc.sync.dma_start(out=out_dram[j], in_=result[:])
 
         grouped_of = {}
-        for i in range(len(halves) + 1):
+        for i in range(len(halves) + LAG):
             if i < len(halves):
-                grouped_of[i] = begin(*halves[i])
-            if i > 0:
-                operand, n, j, half = halves[i - 1]
-                if operand == "x":
-                    finish_x(n, j, half, grouped_of[i - 1])
+                operand, n, j, half = halves[i]
+                if operand == "dy" and half == 0:
+                    mask, scaled = dy_factors(n, j)
+            if i >= LAG:
+                if halves[i - LAG][0] == "x":
+                    finish_x(*halves[i - LAG][1:], grouped_of[i - LAG])
                 else:
-                    finish_dy(n, j, half, grouped_of[i - 1])
+                    finish_dy(*halves[i - LAG][1:], grouped_of[i - LAG])
+            if i < len(halves):
+                if operand == "x":
+                    words = x_raw[(n, j)][:].bitcast(F32)[:, half * BANK_WORDS : (half + 1) * BANK_WORDS]
+                else:
+                    cols = slice(half * HALF_TOKENS, (half + 1) * HALF_TOKENS)
+                    dy = work.tile([P, HALF_TOKENS], BF16, name="dy")
+                    nc.vector.tensor_mul(out=dy[:], in0=scaled[:, cols], in1=mask[:, cols])
+                    words = dy[:].bitcast(F32)
+                grouped_of[i] = turn(words)

@@ -81,22 +81,25 @@ def tile_prefusioncat_v_kernel(
         def load_x(n, j):
             x_raw[(n, j)] = raw.tile([P, TOKENS], BF16, name="x_raw")
             nc.sync.dma_start(out=x_raw[(n, j)][:], in_=x_dram[n, j])
-            halves.extend([("x", n, j, half) for half in range(HALVES)])
+            halves.extend([("x", n, j, half, 0) for half in range(HALVES)])
 
-        def load_dy_inputs(n, j):
+        def load_dy_inputs(n, j, halves_a_load):
             z_raw[(n, j)] = raw.tile([P, TOKENS], F32, name="z_raw")
-            nc.sync.dma_start(out=z_raw[(n, j)][:], in_=z_dram[n, j])
             g_raw[(n, j)] = raw.tile([P, TOKENS], BF16, name="g_raw")
-            nc.sync.dma_start(out=g_raw[(n, j)][:], in_=g_dram[n, 1, j])
-            halves.extend([("dy", n, j, half) for half in range(HALVES)])
+            for first in range(0, HALVES, halves_a_load):
+                cols = slice(first * HALF_TOKENS, (first + halves_a_load) * HALF_TOKENS)
+                nc.sync.dma_start(out=z_raw[(n, j)][:, cols], in_=z_dram[n, j][:, cols])
+                nc.sync.dma_start(out=g_raw[(n, j)][:, cols], in_=g_dram[n, 1, j][:, cols])
+                halves.append(("dy", n, j, first, halves_a_load))
+                halves.extend([("dy", n, j, first + h, 0) for h in range(1, halves_a_load)])
 
         for j in range(TILES):
             load_x(0, j)
         for j in range(TILES):
-            load_dy_inputs(0, j)
+            load_dy_inputs(0, j, HALVES)
             load_x(1, j)
         for j in range(TILES):
-            load_dy_inputs(1, j)
+            load_dy_inputs(1, j, HALVES if j < TILES - 1 else 1)
 
         identity = const.tile([P, P], F32, name="identity")
         make_identity(nc, identity[:])
@@ -114,20 +117,28 @@ def tile_prefusioncat_v_kernel(
         x_scales = const.tile([P, IMAGES * PASSES, CHANNELS], U8, name="x_scales", align_bytes=64)
         acc = [sums.tile([P, CHANNELS], F32, name="acc%d" % j) for j in range(TILES)]
 
-        def dy_factors(n, j):
-            mask = work.tile([P, TOKENS], BF16, name="mask")
+        mask_of = {}
+        scaled_of = {}
+
+        def dy_factors(n, j, half, count):
+            cols = slice(half * HALF_TOKENS, (half + count) * HALF_TOKENS)
+            if half == 0:
+                mask_of[(n, j)] = work.tile([P, TOKENS], BF16, name="mask")
+                scaled_of[(n, j)] = work.tile([P, TOKENS], BF16, name="scaled")
             nc.vector.tensor_scalar(
-                out=mask[:], in0=z_raw[(n, j)][:], scalar1=0.0, scalar2=None, op0=ALU.is_gt
+                out=mask_of[(n, j)][:, cols],
+                in0=z_raw[(n, j)][:, cols],
+                scalar1=0.0,
+                scalar2=None,
+                op0=ALU.is_gt,
             )
-            scaled = work.tile([P, TOKENS], BF16, name="scaled")
             nc.vector.tensor_scalar(
-                out=scaled[:],
-                in0=g_raw[(n, j)][:],
+                out=scaled_of[(n, j)][:, cols],
+                in0=g_raw[(n, j)][:, cols],
                 scalar1=scale[:, j : j + 1],
                 scalar2=None,
                 op0=ALU.mult,
             )
-            return mask, scaled
 
         def turn(words):
             bank = banks.tile([P, BANK_WORDS], F32, name="bank")
@@ -176,20 +187,22 @@ def tile_prefusioncat_v_kernel(
         grouped_of = {}
         for i in range(len(halves) + LAG):
             if i < len(halves):
-                operand, n, j, half = halves[i]
-                if operand == "dy" and half == 0:
-                    mask, scaled = dy_factors(n, j)
+                operand, n, j, half, arriving = halves[i]
+                if arriving > 0:
+                    dy_factors(n, j, half, arriving)
             if i >= LAG:
                 if halves[i - LAG][0] == "x":
-                    finish_x(*halves[i - LAG][1:], grouped_of[i - LAG])
+                    finish_x(*halves[i - LAG][1:4], grouped_of[i - LAG])
                 else:
-                    finish_dy(*halves[i - LAG][1:], grouped_of[i - LAG])
+                    finish_dy(*halves[i - LAG][1:4], grouped_of[i - LAG])
             if i < len(halves):
                 if operand == "x":
                     words = x_raw[(n, j)][:].bitcast(F32)[:, half * BANK_WORDS : (half + 1) * BANK_WORDS]
                 else:
                     cols = slice(half * HALF_TOKENS, (half + 1) * HALF_TOKENS)
                     dy = work.tile([P, HALF_TOKENS], BF16, name="dy")
-                    nc.vector.tensor_mul(out=dy[:], in0=scaled[:, cols], in1=mask[:, cols])
+                    nc.vector.tensor_mul(
+                        out=dy[:], in0=scaled_of[(n, j)][:, cols], in1=mask_of[(n, j)][:, cols]
+                    )
                     words = dy[:].bitcast(F32)
                 grouped_of[i] = turn(words)

@@ -10,20 +10,22 @@ U8 = mybir.dt.uint8
 E4M3_X4 = mybir.dt.float8_e4m3fn_x4
 E5M2_X4 = mybir.dt.float8_e5m2_x4
 ALU = mybir.AluOpType
+ACT = mybir.ActivationFunctionType
 
 P = 128
 IMAGES = 2
 CHANNELS = 512
 TOKENS = 2048
 TILES = CHANNELS // P
+PAIR = 2
 K_PASS = 4 * P
 PASSES = TOKENS // K_PASS
+PASS_WORDS = K_PASS // 2
 BANK_WORDS = 512
-HALF_TOKENS = 2 * BANK_WORDS
-HALF_PASSES = HALF_TOKENS // K_PASS
-HALVES = TOKENS // HALF_TOKENS
+BANK_PASSES = BANK_WORDS // PASS_WORDS
 BN_EPS = 1e-5
-LAG = 4
+WORK = {"x": 2, "dy": 3}
+LAG = 7
 
 FLOPS = 2 * CHANNELS * CHANNELS * IMAGES * TOKENS
 BYTES = IMAGES * CHANNELS * TOKENS * (2 + 2 + 4) + 2 * CHANNELS * 2 + CHANNELS * CHANNELS * 4
@@ -63,8 +65,8 @@ def tile_prefusioncat_v_kernel(
         ctx.enter_context(tc.manual_schedule())
         const = ctx.enter_context(tc.tile_pool(name="const", bufs=1))
         raw = ctx.enter_context(tc.tile_pool(name="raw", bufs=IMAGES * TILES))
-        work = ctx.enter_context(tc.tile_pool(name="work", bufs=3))
-        lagged = ctx.enter_context(tc.tile_pool(name="lagged", bufs=LAG + 2))
+        work = ctx.enter_context(tc.tile_pool(name="work", bufs=4))
+        lagged = ctx.enter_context(tc.tile_pool(name="lagged", bufs=5))
         banks = ctx.enter_context(tc.psum_pool(name="banks", bufs=4))
         sums = ctx.enter_context(tc.psum_pool(name="sums", bufs=1))
 
@@ -76,30 +78,38 @@ def tile_prefusioncat_v_kernel(
         x_raw = {}
         z_raw = {}
         g_raw = {}
-        halves = []
+
+        def tokens_of(first, count):
+            return slice(first * K_PASS, (first + count) * K_PASS)
+
+        steps = []
 
         def load_x(n, j):
-            x_raw[(n, j)] = raw.tile([P, TOKENS], BF16, name="x_raw")
-            nc.sync.dma_start(out=x_raw[(n, j)][:], in_=x_dram[n, j])
-            halves.extend([("x", n, j, half, 0) for half in range(HALVES)])
+            for m in range(j, j + PAIR):
+                x_raw[(n, m)] = raw.tile([P, TOKENS], BF16, name="x_raw")
+                nc.sync.dma_start(out=x_raw[(n, m)][:], in_=x_dram[n, m])
+            for first in range(0, PASSES, BANK_PASSES):
+                steps.extend([("x", n, m, first, BANK_PASSES) for m in range(j, j + PAIR)])
 
-        def load_dy_inputs(n, j, halves_a_load):
+        def load_dy_inputs(n, j, pieces):
             z_raw[(n, j)] = raw.tile([P, TOKENS], F32, name="z_raw")
             g_raw[(n, j)] = raw.tile([P, TOKENS], BF16, name="g_raw")
-            for first in range(0, HALVES, halves_a_load):
-                cols = slice(first * HALF_TOKENS, (first + halves_a_load) * HALF_TOKENS)
-                nc.sync.dma_start(out=z_raw[(n, j)][:, cols], in_=z_dram[n, j][:, cols])
+            for first, count in pieces:
+                cols = tokens_of(first, count)
                 nc.sync.dma_start(out=g_raw[(n, j)][:, cols], in_=g_dram[n, 1, j][:, cols])
-                halves.append(("dy", n, j, first, halves_a_load))
-                halves.extend([("dy", n, j, first + h, 0) for h in range(1, halves_a_load)])
+                nc.sync.dma_start(out=z_raw[(n, j)][:, cols], in_=z_dram[n, j][:, cols])
+                steps.append(("dy", n, j, first, count))
 
-        for j in range(TILES):
+        halves = [(first, BANK_PASSES) for first in range(0, PASSES, BANK_PASSES)]
+        taper = halves[:-1] + [(first, 1) for first in range(PASSES - BANK_PASSES, PASSES)]
+        for j in range(0, TILES, PAIR):
             load_x(0, j)
         for j in range(TILES):
-            load_dy_inputs(0, j, HALVES)
-            load_x(1, j)
+            load_dy_inputs(0, j, halves)
+            if j < TILES // PAIR:
+                load_x(1, j * PAIR)
         for j in range(TILES):
-            load_dy_inputs(1, j, HALVES if j < TILES - 1 else 1)
+            load_dy_inputs(1, j, halves if j < TILES - 1 else taper)
 
         identity = const.tile([P, P], F32, name="identity")
         make_identity(nc, identity[:])
@@ -115,94 +125,134 @@ def tile_prefusioncat_v_kernel(
 
         x_codes = const.tile([P, IMAGES * PASSES, CHANNELS], U32, name="x_codes", align_bytes=64)
         x_scales = const.tile([P, IMAGES * PASSES, CHANNELS], U8, name="x_scales", align_bytes=64)
+        dy_codes = const.tile([P, TILES, IMAGES * PASSES * P], U32, name="dy_codes", align_bytes=64)
+        dy_scales = const.tile([P, TILES, IMAGES * PASSES * P], U8, name="dy_scales", align_bytes=64)
         acc = [sums.tile([P, CHANNELS], F32, name="acc%d" % j) for j in range(TILES)]
 
-        mask_of = {}
         scaled_of = {}
 
-        def dy_factors(n, j, half, count):
-            cols = slice(half * HALF_TOKENS, (half + count) * HALF_TOKENS)
-            if half == 0:
-                mask_of[(n, j)] = work.tile([P, TOKENS], BF16, name="mask")
-                scaled_of[(n, j)] = work.tile([P, TOKENS], BF16, name="scaled")
-            nc.vector.tensor_scalar(
-                out=mask_of[(n, j)][:, cols],
-                in0=z_raw[(n, j)][:, cols],
-                scalar1=0.0,
-                scalar2=None,
-                op0=ALU.is_gt,
-            )
-            nc.vector.tensor_scalar(
-                out=scaled_of[(n, j)][:, cols],
-                in0=g_raw[(n, j)][:, cols],
-                scalar1=scale[:, j : j + 1],
-                scalar2=None,
-                op0=ALU.mult,
-            )
+        def scale_g(n, j, first, count):
+            cols = tokens_of(first, count)
+            scaled_of[(n, j, first)] = work.tile([P, count * K_PASS], BF16, name="scaled")
+            if n == 0:
+                nc.vector.tensor_scalar(
+                    out=scaled_of[(n, j, first)][:],
+                    in0=g_raw[(n, j)][:, cols],
+                    scalar1=scale[:, j : j + 1],
+                    scalar2=None,
+                    op0=ALU.mult,
+                )
+            else:
+                nc.scalar.activation(
+                    out=scaled_of[(n, j, first)][:],
+                    in_=g_raw[(n, j)][:, cols],
+                    func=ACT.Copy,
+                    scale=scale[:, j : j + 1],
+                )
 
-        def turn(words):
+        def turn(words, grouped):
             bank = banks.tile([P, BANK_WORDS], F32, name="bank")
-            for s in range(BANK_WORDS // P):
+            slices = words.shape[1] // P
+            for s in range(slices):
                 nc.tensor.transpose(
                     bank[:, s * P : (s + 1) * P], words[:, s * P : (s + 1) * P], identity[:]
                 )
-            grouped = lagged.tile([P, HALF_TOKENS], BF16, name="grouped", align_bytes=64)
             nc.scalar.copy(
-                out=grouped[:].bitcast(F32).rearrange("p (g c u) -> p g c u", g=HALF_PASSES, u=2),
-                in_=bank[:].rearrange("p (g u c) -> p g c u", g=HALF_PASSES, u=2),
+                out=grouped,
+                in_=bank[:, : slices * P].rearrange("p (g u c) -> p g c u", g=slices // 2, u=2),
             )
-            return grouped
 
-        def finish_x(n, j, half, grouped):
-            for g in range(HALF_PASSES):
-                k = n * PASSES + half * HALF_PASSES + g
+        def finish_x(n, j, first, count, grouped):
+            for g in range(count):
+                k = n * PASSES + first + g
+                cols = slice(j * P, (j + PAIR) * P)
                 nc.vector.quantize_mx(
-                    out=x_codes[:, k, j * P : (j + 1) * P].bitcast(E4M3_X4),
-                    scales=x_scales[:, k, j * P : (j + 1) * P],
-                    in_=grouped[:, g * 4 * P : (g + 1) * 4 * P],
+                    out=x_codes[:, k, cols].bitcast(E4M3_X4),
+                    scales=x_scales[:, k, cols],
+                    in_=grouped[:, g * PAIR * 4 * P : (g + 1) * PAIR * 4 * P],
                 )
 
-        def finish_dy(n, j, half, grouped):
-            dy_codes = work.tile([P, HALF_PASSES * P], U32, name="dy_codes", align_bytes=64)
-            dy_scales = work.tile([P, HALF_PASSES * P], U8, name="dy_scales", align_bytes=64)
+        def finish_dy(n, j, first, count, grouped):
+            cols = slice((n * PASSES + first) * P, (n * PASSES + first + count) * P)
             nc.vector.quantize_mx(
-                out=dy_codes[:].bitcast(E5M2_X4), scales=dy_scales[:], in_=grouped[:]
+                out=dy_codes[:, j, cols].bitcast(E5M2_X4),
+                scales=dy_scales[:, j, cols],
+                in_=grouped[:],
             )
-            for g in range(HALF_PASSES):
-                k = n * PASSES + half * HALF_PASSES + g
+
+        def multiply(n, j, first, count):
+            for k in range(n * PASSES + first, n * PASSES + first + count):
+                cols = slice(k * P, (k + 1) * P)
                 nc.tensor.matmul_mx(
                     out=acc[j][:],
-                    lhsT=dy_codes[:, g * P : (g + 1) * P].bitcast(E5M2_X4),
-                    lhsT_scale=dy_scales[:, g * P : (g + 1) * P],
+                    lhsT=dy_codes[:, j, cols].bitcast(E5M2_X4),
+                    lhsT_scale=dy_scales[:, j, cols],
                     rhs=x_codes[:, k, :].bitcast(E4M3_X4),
                     rhs_scale=x_scales[:, k, :],
                     start=(k == 0),
                     stop=(k == IMAGES * PASSES - 1),
                 )
-            if n == IMAGES - 1 and half == HALVES - 1:
+            if n == IMAGES - 1 and first + count == PASSES:
                 result = work.tile([P, CHANNELS], F32, name="result")
                 nc.scalar.copy(out=result[:], in_=acc[j][:])
                 nc.sync.dma_start(out=out_dram[j], in_=result[:])
 
-        grouped_of = {}
-        for i in range(len(halves) + LAG):
-            if i < len(halves):
-                operand, n, j, half, arriving = halves[i]
-                if arriving > 0:
-                    dy_factors(n, j, half, arriving)
-            if i >= LAG:
-                if halves[i - LAG][0] == "x":
-                    finish_x(*halves[i - LAG][1:4], grouped_of[i - LAG])
-                else:
-                    finish_dy(*halves[i - LAG][1:4], grouped_of[i - LAG])
-            if i < len(halves):
-                if operand == "x":
-                    words = x_raw[(n, j)][:].bitcast(F32)[:, half * BANK_WORDS : (half + 1) * BANK_WORDS]
-                else:
-                    cols = slice(half * HALF_TOKENS, (half + 1) * HALF_TOKENS)
-                    dy = work.tile([P, HALF_TOKENS], BF16, name="dy")
-                    nc.vector.tensor_mul(
-                        out=dy[:], in0=scaled_of[(n, j)][:, cols], in1=mask_of[(n, j)][:, cols]
+        turned = []
+        waiting = []
+        x_passes_done = [0] * IMAGES
+        begun = 0
+
+        def finish_oldest():
+            operand, n, j, first, count, grouped = turned[0][1:]
+            turned.remove(turned[0])
+            if operand == "x":
+                finish_x(n, j, first, count, grouped)
+                x_passes_done[n] += count
+            else:
+                finish_dy(n, j, first, count, grouped)
+                waiting.append((n, j, first, count))
+            if waiting and x_passes_done[waiting[0][0]] == PASSES * TILES // PAIR:
+                multiply(*waiting[0])
+                waiting.remove(waiting[0])
+
+        for i, (operand, n, j, first, count) in enumerate(steps):
+            if operand == "dy":
+                cols = tokens_of(first, count)
+                mask = work.tile([P, count * K_PASS], BF16, name="mask")
+                nc.vector.tensor_scalar(
+                    out=mask[:], in0=z_raw[(n, j)][:, cols], scalar1=0.0, scalar2=None, op0=ALU.is_gt
+                )
+                if (n, j, first) not in scaled_of:
+                    scale_g(n, j, first, count)
+            for ahead in (1, 2):
+                if i + ahead < len(steps) and steps[i + ahead][0] == "dy":
+                    if steps[i + ahead][1:4] not in scaled_of and (ahead == 1 or steps[i + ahead][1] > 0):
+                        scale_g(*steps[i + ahead][1:])
+            if turned and begun - turned[0][0] >= LAG:
+                finish_oldest()
+            if operand == "dy":
+                dy = work.tile([P, count * K_PASS], BF16, name="dy")
+                nc.vector.tensor_mul(out=dy[:], in0=scaled_of[(n, j, first)][:], in1=mask[:])
+                grouped = lagged.tile([P, count * K_PASS], BF16, name="grouped", align_bytes=64)
+                turn(
+                    dy[:].bitcast(F32),
+                    grouped[:].bitcast(F32).rearrange("p (g c u) -> p g c u", g=count, u=2),
+                )
+            else:
+                if j % PAIR == 0:
+                    x_grouped = lagged.tile(
+                        [P, count * PAIR * K_PASS], BF16, name="x_grouped", align_bytes=64
                     )
-                    words = dy[:].bitcast(F32)
-                grouped_of[i] = turn(words)
+                turn(
+                    x_raw[(n, j)][:, tokens_of(first, count)].bitcast(F32),
+                    x_grouped[:]
+                    .bitcast(F32)
+                    .rearrange("p (g m c u) -> p m g c u", g=count, m=PAIR, u=2)[:, j % PAIR],
+                )
+            begun += WORK[operand]
+            if operand == "dy":
+                turned.append((begun, operand, n, j, first, count, grouped))
+            elif j % PAIR == PAIR - 1:
+                turned.append((begun, operand, n, j - PAIR + 1, first, count, x_grouped))
+        while turned:
+            finish_oldest()

@@ -91,25 +91,29 @@ def tile_prefusioncat_v_kernel(
             for first in range(0, PASSES, BANK_PASSES):
                 steps.extend([("x", n, m, first, BANK_PASSES) for m in range(j, j + PAIR)])
 
-        def load_dy_inputs(n, j, pieces):
-            z_raw[(n, j)] = raw.tile([P, TOKENS], F32, name="z_raw")
+        def load_dy_inputs(n, j, pieces, loads):
             g_raw[(n, j)] = raw.tile([P, TOKENS], BF16, name="g_raw")
-            for first, count in pieces:
+            nc.sync.dma_start(out=g_raw[(n, j)][:], in_=g_dram[n, 1, j])
+            z_raw[(n, j)] = raw.tile([P, TOKENS], F32, name="z_raw")
+            for first, count in loads:
                 cols = tokens_of(first, count)
-                nc.sync.dma_start(out=g_raw[(n, j)][:, cols], in_=g_dram[n, 1, j][:, cols])
                 nc.sync.dma_start(out=z_raw[(n, j)][:, cols], in_=z_dram[n, j][:, cols])
-                steps.append(("dy", n, j, first, count))
+            steps.extend([("dy", n, j, first, count) for first, count in pieces])
 
+        whole = [(0, PASSES)]
         halves = [(first, BANK_PASSES) for first in range(0, PASSES, BANK_PASSES)]
         taper = halves[:-1] + [(first, 1) for first in range(PASSES - BANK_PASSES, PASSES)]
         for j in range(0, TILES, PAIR):
             load_x(0, j)
         for j in range(TILES):
-            load_dy_inputs(0, j, halves)
+            load_dy_inputs(0, j, halves, whole)
             if j < TILES // PAIR:
                 load_x(1, j * PAIR)
         for j in range(TILES):
-            load_dy_inputs(1, j, halves if j < TILES - 1 else taper)
+            if j < TILES - 1:
+                load_dy_inputs(1, j, halves, whole)
+            else:
+                load_dy_inputs(1, j, taper, taper)
 
         identity = const.tile([P, P], F32, name="identity")
         make_identity(nc, identity[:])

@@ -24,8 +24,8 @@ PASS_WORDS = K_PASS // 2
 BANK_WORDS = 512
 BANK_PASSES = BANK_WORDS // PASS_WORDS
 BN_EPS = 1e-5
-WORK = {"x": 2, "dy": 3}
-LAG = 7
+WORK = {"x": 1, "dy": 2}
+LAG = 4
 
 FLOPS = 2 * CHANNELS * CHANNELS * IMAGES * TOKENS
 BYTES = IMAGES * CHANNELS * TOKENS * (2 + 2 + 4) + 2 * CHANNELS * 2 + CHANNELS * CHANNELS * 4
@@ -56,7 +56,7 @@ def tile_prefusioncat_v_kernel(
     out,
 ):
     nc = tc.nc
-    x_dram = pts_feat0.rearrange("n (j p) h w -> n j p (h w)", p=P)
+    x_dram = pts_feat0.rearrange("n (p j) h w -> n p j (h w)", j=TILES)
     z_dram = pts_z.rearrange("n (p j) h w -> n j p (h w)", j=TILES)
     g_dram = grad_out.rearrange("n (s p j) h w -> n s j p (h w)", s=2, j=TILES)
     out_dram = out.rearrange("(p j) c -> j p c", j=TILES)
@@ -65,16 +65,14 @@ def tile_prefusioncat_v_kernel(
         ctx.enter_context(tc.manual_schedule())
         const = ctx.enter_context(tc.tile_pool(name="const", bufs=1))
         raw = ctx.enter_context(tc.tile_pool(name="raw", bufs=IMAGES * TILES))
+        pairs = ctx.enter_context(tc.tile_pool(name="pairs", bufs=IMAGES * TILES // PAIR))
         work = ctx.enter_context(tc.tile_pool(name="work", bufs=4))
         lagged = ctx.enter_context(tc.tile_pool(name="lagged", bufs=5))
         banks = ctx.enter_context(tc.psum_pool(name="banks", bufs=4))
         sums = ctx.enter_context(tc.psum_pool(name="sums", bufs=1))
 
         var = const.tile([P, TILES], BF16, name="var")
-        nc.sync.dma_start(out=var[:], in_=pts_var.rearrange("(p j) -> p j", j=TILES))
         gamma = const.tile([P, TILES], BF16, name="gamma")
-        nc.sync.dma_start(out=gamma[:], in_=pts_gamma.rearrange("(p j) -> p j", j=TILES))
-
         x_raw = {}
         z_raw = {}
         g_raw = {}
@@ -85,9 +83,8 @@ def tile_prefusioncat_v_kernel(
         steps = []
 
         def load_x(n, j):
-            for m in range(j, j + PAIR):
-                x_raw[(n, m)] = raw.tile([P, TOKENS], BF16, name="x_raw")
-                nc.sync.dma_start(out=x_raw[(n, m)][:], in_=x_dram[n, m])
+            x_raw[(n, j)] = pairs.tile([P, PAIR, TOKENS], BF16, name="x_raw")
+            nc.sync.dma_start(out=x_raw[(n, j)][:], in_=x_dram[n, :, j : j + PAIR])
             for first in range(0, PASSES, BANK_PASSES):
                 steps.extend([("x", n, m, first, BANK_PASSES) for m in range(j, j + PAIR)])
 
@@ -103,29 +100,34 @@ def tile_prefusioncat_v_kernel(
         whole = [(0, PASSES)]
         halves = [(first, BANK_PASSES) for first in range(0, PASSES, BANK_PASSES)]
         taper = halves[:-1] + [(first, 1) for first in range(PASSES - BANK_PASSES, PASSES)]
-        for j in range(0, TILES, PAIR):
-            load_x(0, j)
-        for j in range(TILES):
-            load_dy_inputs(0, j, halves, whole)
-            if j < TILES // PAIR:
-                load_x(1, j * PAIR)
-        for j in range(TILES):
-            if j < TILES - 1:
-                load_dy_inputs(1, j, halves, whole)
+        dy_tiles = [(n, j) for n in range(IMAGES) for j in range(TILES)]
+        x_pairs = [(n, j) for n in range(IMAGES) for j in range(0, TILES, PAIR)]
+        for i, (n, j) in enumerate(dy_tiles):
+            if i < len(x_pairs):
+                load_x(*x_pairs[i])
+            if i == 0:
+                nc.sync.dma_start(out=var[:], in_=pts_var.rearrange("(p j) -> p j", j=TILES))
+                nc.sync.dma_start(out=gamma[:], in_=pts_gamma.rearrange("(p j) -> p j", j=TILES))
+            if i < len(dy_tiles) - 2:
+                load_dy_inputs(n, j, halves, whole)
+            elif i == len(dy_tiles) - 2:
+                load_dy_inputs(n, j, halves, halves)
             else:
-                load_dy_inputs(1, j, taper, taper)
+                load_dy_inputs(n, j, taper, taper)
 
         identity = const.tile([P, P], F32, name="identity")
         make_identity(nc, identity[:])
 
+        minus_half = const.tile([P, TILES], F32, name="minus_half")
+        nc.gpsimd.memset(minus_half[:], -0.5)
         var_eps = const.tile([P, TILES], F32, name="var_eps")
-        nc.vector.tensor_scalar_add(out=var_eps[:], in0=var[:], scalar1=BN_EPS)
-        std = const.tile([P, TILES], F32, name="std")
-        nc.scalar.sqrt(out=std[:], in_=var_eps[:])
+        nc.gpsimd.tensor_scalar(
+            out=var_eps[:], in0=var[:], scalar1=BN_EPS, scalar2=None, op0=ALU.add
+        )
         inv_std = const.tile([P, TILES], F32, name="inv_std")
-        nc.vector.reciprocal(out=inv_std[:], in_=std[:])
+        nc.gpsimd.tensor_tensor(out=inv_std[:], in0=var_eps[:], in1=minus_half[:], op=ALU.pow)
         scale = const.tile([P, TILES], F32, name="scale")
-        nc.vector.tensor_mul(out=scale[:], in0=gamma[:], in1=inv_std[:])
+        nc.gpsimd.tensor_mul(out=scale[:], in0=gamma[:], in1=inv_std[:])
 
         x_codes = const.tile([P, IMAGES * PASSES, CHANNELS], U32, name="x_codes", align_bytes=64)
         x_scales = const.tile([P, IMAGES * PASSES, CHANNELS], U8, name="x_scales", align_bytes=64)
@@ -135,10 +137,13 @@ def tile_prefusioncat_v_kernel(
 
         scaled_of = {}
 
+        def on_scalar(n, j):
+            return n == IMAGES - 1 and j < TILES - 1
+
         def scale_g(n, j, first, count):
             cols = tokens_of(first, count)
             scaled_of[(n, j, first)] = work.tile([P, count * K_PASS], BF16, name="scaled")
-            if n == 0:
+            if not on_scalar(n, j):
                 nc.vector.tensor_scalar(
                     out=scaled_of[(n, j, first)][:],
                     in0=g_raw[(n, j)][:, cols],
@@ -184,6 +189,8 @@ def tile_prefusioncat_v_kernel(
                 in_=grouped[:],
             )
 
+        summed = []
+
         def multiply(n, j, first, count):
             for k in range(n * PASSES + first, n * PASSES + first + count):
                 cols = slice(k * P, (k + 1) * P)
@@ -197,9 +204,17 @@ def tile_prefusioncat_v_kernel(
                     stop=(k == IMAGES * PASSES - 1),
                 )
             if n == IMAGES - 1 and first + count == PASSES:
+                summed.append(j)
+
+        def store_summed():
+            for j in summed:
                 result = work.tile([P, CHANNELS], F32, name="result")
-                nc.scalar.copy(out=result[:], in_=acc[j][:])
+                nc.scalar.copy(
+                    out=result[:].rearrange("o (p m) -> o p m", m=TILES),
+                    in_=acc[j][:].rearrange("o (m p) -> o p m", m=TILES),
+                )
                 nc.sync.dma_start(out=out_dram[j], in_=result[:])
+            summed.clear()
 
         turned = []
         waiting = []
@@ -222,21 +237,36 @@ def tile_prefusioncat_v_kernel(
         for i, (operand, n, j, first, count) in enumerate(steps):
             if operand == "dy":
                 cols = tokens_of(first, count)
-                mask = work.tile([P, count * K_PASS], BF16, name="mask")
-                nc.vector.tensor_scalar(
-                    out=mask[:], in0=z_raw[(n, j)][:, cols], scalar1=0.0, scalar2=None, op0=ALU.is_gt
-                )
+                if count > 1:
+                    mask = work.tile([P, count * K_PASS], BF16, name="mask")
+                    nc.vector.tensor_scalar(
+                        out=mask[:],
+                        in0=z_raw[(n, j)][:, cols],
+                        scalar1=0.0,
+                        scalar2=None,
+                        op0=ALU.is_gt,
+                    )
                 if (n, j, first) not in scaled_of:
                     scale_g(n, j, first, count)
             for ahead in (1, 2):
                 if i + ahead < len(steps) and steps[i + ahead][0] == "dy":
-                    if steps[i + ahead][1:4] not in scaled_of and (ahead == 1 or steps[i + ahead][1] > 0):
+                    if steps[i + ahead][1:4] not in scaled_of and (ahead == 1 or on_scalar(*steps[i + ahead][1:3])):
                         scale_g(*steps[i + ahead][1:])
             if turned and begun - turned[0][0] >= LAG:
                 finish_oldest()
             if operand == "dy":
                 dy = work.tile([P, count * K_PASS], BF16, name="dy")
-                nc.vector.tensor_mul(out=dy[:], in0=scaled_of[(n, j, first)][:], in1=mask[:])
+                if count > 1:
+                    nc.vector.tensor_mul(out=dy[:], in0=scaled_of[(n, j, first)][:], in1=mask[:])
+                else:
+                    nc.vector.scalar_tensor_tensor(
+                        out=dy[:],
+                        in0=z_raw[(n, j)][:, cols],
+                        scalar=0.0,
+                        in1=scaled_of[(n, j, first)][:],
+                        op0=ALU.is_gt,
+                        op1=ALU.mult,
+                    )
                 grouped = lagged.tile([P, count * K_PASS], BF16, name="grouped", align_bytes=64)
                 turn(
                     dy[:].bitcast(F32),
@@ -248,11 +278,12 @@ def tile_prefusioncat_v_kernel(
                         [P, count * PAIR * K_PASS], BF16, name="x_grouped", align_bytes=64
                     )
                 turn(
-                    x_raw[(n, j)][:, tokens_of(first, count)].bitcast(F32),
+                    x_raw[(n, j - j % PAIR)][:, j % PAIR, tokens_of(first, count)].bitcast(F32),
                     x_grouped[:]
                     .bitcast(F32)
                     .rearrange("p (g m c u) -> p m g c u", g=count, m=PAIR, u=2)[:, j % PAIR],
                 )
+            store_summed()
             begun += WORK[operand]
             if operand == "dy":
                 turned.append((begun, operand, n, j, first, count, grouped))
@@ -260,3 +291,4 @@ def tile_prefusioncat_v_kernel(
                 turned.append((begun, operand, n, j - PAIR + 1, first, count, x_grouped))
         while turned:
             finish_oldest()
+            store_summed()

@@ -103,11 +103,12 @@ def tile_prefusioncat_v_kernel(
         dy_tiles = [(n, j) for n in range(IMAGES) for j in range(TILES)]
         x_pairs = [(n, j) for n in range(IMAGES) for j in range(0, TILES, PAIR)]
         for i, (n, j) in enumerate(dy_tiles):
-            if i < len(x_pairs):
-                load_x(*x_pairs[i])
             if i == 0:
+                load_x(*x_pairs[0])
                 nc.sync.dma_start(out=var[:], in_=pts_var.rearrange("(p j) -> p j", j=TILES))
                 nc.sync.dma_start(out=gamma[:], in_=pts_gamma.rearrange("(p j) -> p j", j=TILES))
+            if i + 1 < len(x_pairs):
+                load_x(*x_pairs[i + 1])
             if i < len(dy_tiles) - 2:
                 load_dy_inputs(n, j, halves, whole)
             elif i == len(dy_tiles) - 2:
@@ -138,7 +139,7 @@ def tile_prefusioncat_v_kernel(
         scaled_of = {}
 
         def on_scalar(n, j):
-            return n == IMAGES - 1 and j < TILES - 1
+            return len(x_pairs) - 1 <= n * TILES + j < len(dy_tiles) - 1
 
         def scale_g(n, j, first, count):
             cols = tokens_of(first, count)
@@ -208,12 +209,18 @@ def tile_prefusioncat_v_kernel(
 
         def store_summed():
             for j in summed:
-                result = work.tile([P, CHANNELS], F32, name="result")
-                nc.scalar.copy(
-                    out=result[:].rearrange("o (p m) -> o p m", m=TILES),
-                    in_=acc[j][:].rearrange("o (m p) -> o p m", m=TILES),
-                )
-                nc.sync.dma_start(out=out_dram[j], in_=result[:])
+                parts = 1 if j < TILES - 1 else 2
+                channels = CHANNELS // parts
+                sums_of = acc[j][:].rearrange("o (m p) -> o p m", m=TILES)
+                for part in range(parts):
+                    result = work.tile([P, channels], F32, name="result")
+                    nc.scalar.copy(
+                        out=result[:].rearrange("o (p m) -> o p m", m=TILES),
+                        in_=sums_of[:, part * P // parts : (part + 1) * P // parts],
+                    )
+                    nc.sync.dma_start(
+                        out=out_dram[j][:, part * channels : (part + 1) * channels], in_=result[:]
+                    )
             summed.clear()
 
         turned = []
@@ -252,7 +259,7 @@ def tile_prefusioncat_v_kernel(
                 if i + ahead < len(steps) and steps[i + ahead][0] == "dy":
                     if steps[i + ahead][1:4] not in scaled_of and (ahead == 1 or on_scalar(*steps[i + ahead][1:3])):
                         scale_g(*steps[i + ahead][1:])
-            if turned and begun - turned[0][0] >= LAG:
+            if i < len(steps) - 1 and turned and begun - turned[0][0] >= LAG:
                 finish_oldest()
             if operand == "dy":
                 dy = work.tile([P, count * K_PASS], BF16, name="dy")

@@ -109,9 +109,9 @@ def tile_prefusioncat_v_kernel(
                 nc.sync.dma_start(out=gamma[:], in_=pts_gamma.rearrange("(p j) -> p j", j=TILES))
             if i + 1 < len(x_pairs):
                 load_x(*x_pairs[i + 1])
-            if i < len(dy_tiles) - 2:
+            if i < len(dy_tiles) - 3:
                 load_dy_inputs(n, j, halves, whole)
-            elif i == len(dy_tiles) - 2:
+            elif i < len(dy_tiles) - 1:
                 load_dy_inputs(n, j, halves, halves)
             else:
                 load_dy_inputs(n, j, taper, taper)
@@ -138,13 +138,15 @@ def tile_prefusioncat_v_kernel(
 
         scaled_of = {}
 
-        def on_scalar(n, j):
-            return len(x_pairs) - 1 <= n * TILES + j < len(dy_tiles) - 1
+        def on_scalar(n, j, first):
+            if (n, j) == dy_tiles[-1]:
+                return first == taper[1][0]
+            return len(x_pairs) - 1 <= n * TILES + j
 
         def scale_g(n, j, first, count):
             cols = tokens_of(first, count)
             scaled_of[(n, j, first)] = work.tile([P, count * K_PASS], BF16, name="scaled")
-            if not on_scalar(n, j):
+            if not on_scalar(n, j, first):
                 nc.vector.tensor_scalar(
                     out=scaled_of[(n, j, first)][:],
                     in0=g_raw[(n, j)][:, cols],
@@ -244,7 +246,7 @@ def tile_prefusioncat_v_kernel(
         for i, (operand, n, j, first, count) in enumerate(steps):
             if operand == "dy":
                 cols = tokens_of(first, count)
-                if count > 1:
+                if (n, j) != dy_tiles[-1]:
                     mask = work.tile([P, count * K_PASS], BF16, name="mask")
                     nc.vector.tensor_scalar(
                         out=mask[:],
@@ -257,13 +259,13 @@ def tile_prefusioncat_v_kernel(
                     scale_g(n, j, first, count)
             for ahead in (1, 2):
                 if i + ahead < len(steps) and steps[i + ahead][0] == "dy":
-                    if steps[i + ahead][1:4] not in scaled_of and (ahead == 1 or on_scalar(*steps[i + ahead][1:3])):
+                    if steps[i + ahead][1:4] not in scaled_of and (ahead == 1 or on_scalar(*steps[i + ahead][1:4])):
                         scale_g(*steps[i + ahead][1:])
             if i < len(steps) - 1 and turned and begun - turned[0][0] >= LAG:
                 finish_oldest()
             if operand == "dy":
                 dy = work.tile([P, count * K_PASS], BF16, name="dy")
-                if count > 1:
+                if (n, j) != dy_tiles[-1]:
                     nc.vector.tensor_mul(out=dy[:], in0=scaled_of[(n, j, first)][:], in1=mask[:])
                 else:
                     nc.vector.scalar_tensor_tensor(

@@ -139,9 +139,8 @@ def tile_prefusioncat_v_kernel(
         scaled_of = {}
 
         def on_scalar(n, j, first):
-            if (n, j) == dy_tiles[-1]:
-                return first == taper[1][0]
-            return len(x_pairs) - 1 <= n * TILES + j
+            behind = n * TILES + j - (len(x_pairs) - 1)
+            return (behind > 0 or behind == 0 and first > 0) and (n, j) != dy_tiles[-1]
 
         def scale_g(n, j, first, count):
             cols = tokens_of(first, count)

@@ -84,7 +84,7 @@ def tile_prefusioncat_v_kernel(
 
         def load_x(n, j):
             x_raw[(n, j)] = pairs.tile([P, PAIR, TOKENS], BF16, name="x_raw")
-            nc.sync.dma_start(out=x_raw[(n, j)][:], in_=x_dram[n, :, j : j + PAIR])
+            nc.scalar.dma_start(out=x_raw[(n, j)][:], in_=x_dram[n, :, j : j + PAIR])
             for first in range(0, PASSES, BANK_PASSES):
                 steps.extend([("x", n, m, first, BANK_PASSES) for m in range(j, j + PAIR)])
 
@@ -242,6 +242,7 @@ def tile_prefusioncat_v_kernel(
                 multiply(*waiting[0])
                 waiting.remove(waiting[0])
 
+        regular = len(steps) - len(taper)
         for i, (operand, n, j, first, count) in enumerate(steps):
             if operand == "dy":
                 cols = tokens_of(first, count)
@@ -291,7 +292,8 @@ def tile_prefusioncat_v_kernel(
                     .bitcast(F32)
                     .rearrange("p (g m c u) -> p m g c u", g=count, m=PAIR, u=2)[:, j % PAIR],
                 )
-            store_summed()
+            if i < regular or i == len(steps) - 1:
+                store_summed()
             begun += WORK[operand]
             if operand == "dy":
                 turned.append((begun, operand, n, j, first, count, grouped))

from contextlib import ExitStack

import concourse.mybir as mybir
from concourse.masks import make_identity

F32 = mybir.dt.float32
BF16 = mybir.dt.bfloat16
U32 = mybir.dt.uint32
U8 = mybir.dt.uint8
E4M3_X4 = mybir.dt.float8_e4m3fn_x4
E5M2_X4 = mybir.dt.float8_e5m2_x4
ALU = mybir.AluOpType
ACT = mybir.ActivationFunctionType

P = 128
IMAGES = 2
CHANNELS = 512
TOKENS = 2048
TILES = CHANNELS // P
PAIR = 2
K_PASS = 4 * P
PASSES = TOKENS // K_PASS
PASS_WORDS = K_PASS // 2
BANK_WORDS = 512
BANK_PASSES = BANK_WORDS // PASS_WORDS
BN_EPS = 1e-5
WORK = {"x": 1, "dy": 2}
LAG = 4

FLOPS = 2 * CHANNELS * CHANNELS * IMAGES * TOKENS
BYTES = IMAGES * CHANNELS * TOKENS * (2 + 2 + 4) + 2 * CHANNELS * 2 + CHANNELS * CHANNELS * 4


def tile_prefusioncat_v_kernel(
    tc,
    img_feat0,
    img_feat1,
    img_feat2,
    img_feat3,
    img_feat4,
    pts_feat0,
    img_w,
    img_b,
    img_gamma,
    img_beta,
    img_mean,
    img_var,
    pts_w,
    pts_b,
    pts_gamma,
    pts_beta,
    pts_mean,
    pts_var,
    pts_z,
    grad_out,
    out,
):
    nc = tc.nc
    x_dram = pts_feat0.rearrange("n (p j) h w -> n p j (h w)", j=TILES)
    z_dram = pts_z.rearrange("n (p j) h w -> n j p (h w)", j=TILES)
    g_dram = grad_out.rearrange("n (s p j) h w -> n s j p (h w)", s=2, j=TILES)
    out_dram = out.rearrange("(p j) c -> j p c", j=TILES)

    with ExitStack() as ctx:
        ctx.enter_context(tc.manual_schedule())
        const = ctx.enter_context(tc.tile_pool(name="const", bufs=1))
        raw = ctx.enter_context(tc.tile_pool(name="raw", bufs=IMAGES * TILES))
        pairs = ctx.enter_context(tc.tile_pool(name="pairs", bufs=IMAGES * TILES // PAIR))
        work = ctx.enter_context(tc.tile_pool(name="work", bufs=4))
        lagged = ctx.enter_context(tc.tile_pool(name="lagged", bufs=5))
        banks = ctx.enter_context(tc.psum_pool(name="banks", bufs=4))
        sums = ctx.enter_context(tc.psum_pool(name="sums", bufs=1))

        var = const.tile([P, TILES], BF16, name="var")
        gamma = const.tile([P, TILES], BF16, name="gamma")
        x_raw = {}
        z_raw = {}
        g_raw = {}

        def tokens_of(first, count):
            return slice(first * K_PASS, (first + count) * K_PASS)

        steps = []

        def load_x(n, j):
            x_raw[(n, j)] = pairs.tile([P, PAIR, TOKENS], BF16, name="x_raw")
            nc.scalar.dma_start(out=x_raw[(n, j)][:], in_=x_dram[n, :, j : j + PAIR])
            for first in range(0, PASSES, BANK_PASSES):
                steps.extend([("x", n, m, first, BANK_PASSES) for m in range(j, j + PAIR)])

        def load_dy_inputs(n, j, pieces, loads):
            g_raw[(n, j)] = raw.tile([P, TOKENS], BF16, name="g_raw")
            nc.sync.dma_start(out=g_raw[(n, j)][:], in_=g_dram[n, 1, j])
            z_raw[(n, j)] = raw.tile([P, TOKENS], F32, name="z_raw")
            for first, count in loads:
                cols = tokens_of(first, count)
                nc.sync.dma_start(out=z_raw[(n, j)][:, cols], in_=z_dram[n, j][:, cols])
            steps.extend([("dy", n, j, first, count) for first, count in pieces])

        whole = [(0, PASSES)]
        halves = [(first, BANK_PASSES) for first in range(0, PASSES, BANK_PASSES)]
        taper = halves[:-1] + [(first, 1) for first in range(PASSES - BANK_PASSES, PASSES)]
        dy_tiles = [(n, j) for n in range(IMAGES) for j in range(TILES)]
        x_pairs = [(n, j) for n in range(IMAGES) for j in range(0, TILES, PAIR)]
        for i, (n, j) in enumerate(dy_tiles):
            if i == 0:
                load_x(*x_pairs[0])
                nc.sync.dma_start(out=var[:], in_=pts_var.rearrange("(p j) -> p j", j=TILES))
                nc.sync.dma_start(out=gamma[:], in_=pts_gamma.rearrange("(p j) -> p j", j=TILES))
            if i + 1 < len(x_pairs):
                load_x(*x_pairs[i + 1])
            if i < len(dy_tiles) - 3:
                load_dy_inputs(n, j, halves, whole)
            elif i < len(dy_tiles) - 1:
                load_dy_inputs(n, j, halves, halves)
            else:
                load_dy_inputs(n, j, taper, taper)

        identity = const.tile([P, P], F32, name="identity")
        make_identity(nc, identity[:])

        minus_half = const.tile([P, TILES], F32, name="minus_half")
        nc.gpsimd.memset(minus_half[:], -0.5)
        var_eps = const.tile([P, TILES], F32, name="var_eps")
        nc.gpsimd.tensor_scalar(
            out=var_eps[:], in0=var[:], scalar1=BN_EPS, scalar2=None, op0=ALU.add
        )
        inv_std = const.tile([P, TILES], F32, name="inv_std")
        nc.gpsimd.tensor_tensor(out=inv_std[:], in0=var_eps[:], in1=minus_half[:], op=ALU.pow)
        scale = const.tile([P, TILES], F32, name="scale")
        nc.gpsimd.tensor_mul(out=scale[:], in0=gamma[:], in1=inv_std[:])

        x_codes = const.tile([P, IMAGES * PASSES, CHANNELS], U32, name="x_codes", align_bytes=64)
        x_scales = const.tile([P, IMAGES * PASSES, CHANNELS], U8, name="x_scales", align_bytes=64)
        dy_codes = const.tile([P, TILES, IMAGES * PASSES * P], U32, name="dy_codes", align_bytes=64)
        dy_scales = const.tile([P, TILES, IMAGES * PASSES * P], U8, name="dy_scales", align_bytes=64)
        acc = [sums.tile([P, CHANNELS], F32, name="acc%d" % j) for j in range(TILES)]

        scaled_of = {}

        def on_scalar(n, j, first):
            behind = n * TILES + j - (len(x_pairs) - 1)
            return (behind > 0 or behind == 0 and first > 0) and (n, j) != dy_tiles[-1]

        def scale_g(n, j, first, count):
            cols = tokens_of(first, count)
            scaled_of[(n, j, first)] = work.tile([P, count * K_PASS], BF16, name="scaled")
            if not on_scalar(n, j, first):
                nc.vector.tensor_scalar(
                    out=scaled_of[(n, j, first)][:],
                    in0=g_raw[(n, j)][:, cols],
                    scalar1=scale[:, j : j + 1],
                    scalar2=None,
                    op0=ALU.mult,
                )
            else:
                nc.scalar.activation(
                    out=scaled_of[(n, j, first)][:],
                    in_=g_raw[(n, j)][:, cols],
                    func=ACT.Copy,
                    scale=scale[:, j : j + 1],
                )

        def turn(words, grouped):
            bank = banks.tile([P, BANK_WORDS], F32, name="bank")
            slices = words.shape[1] // P
            for s in range(slices):
                nc.tensor.transpose(
                    bank[:, s * P : (s + 1) * P], words[:, s * P : (s + 1) * P], identity[:]
                )
            nc.scalar.copy(
                out=grouped,
                in_=bank[:, : slices * P].rearrange("p (g u c) -> p g c u", g=slices // 2, u=2),
            )

        def finish_x(n, j, first, count, grouped):
            for g in range(count):
                k = n * PASSES + first + g
                cols = slice(j * P, (j + PAIR) * P)
                nc.vector.quantize_mx(
                    out=x_codes[:, k, cols].bitcast(E4M3_X4),
                    scales=x_scales[:, k, cols],
                    in_=grouped[:, g * PAIR * 4 * P : (g + 1) * PAIR * 4 * P],
                )

        def finish_dy(n, j, first, count, grouped):
            cols = slice((n * PASSES + first) * P, (n * PASSES + first + count) * P)
            nc.vector.quantize_mx(
                out=dy_codes[:, j, cols].bitcast(E5M2_X4),
                scales=dy_scales[:, j, cols],
                in_=grouped[:],
            )

        summed = []

        def multiply(n, j, first, count):
            for k in range(n * PASSES + first, n * PASSES + first + count):
                cols = slice(k * P, (k + 1) * P)
                nc.tensor.matmul_mx(
                    out=acc[j][:],
                    lhsT=dy_codes[:, j, cols].bitcast(E5M2_X4),
                    lhsT_scale=dy_scales[:, j, cols],
                    rhs=x_codes[:, k, :].bitcast(E4M3_X4),
                    rhs_scale=x_scales[:, k, :],
                    start=(k == 0),
                    stop=(k == IMAGES * PASSES - 1),
                )
            if n == IMAGES - 1 and first + count == PASSES:
                summed.append(j)

        def store_summed():
            for j in summed:
                parts = 1 if j < TILES - 1 else 2
                channels = CHANNELS // parts
                sums_of = acc[j][:].rearrange("o (m p) -> o p m", m=TILES)
                for part in range(parts):
                    result = work.tile([P, channels], F32, name="result")
                    nc.scalar.copy(
                        out=result[:].rearrange("o (p m) -> o p m", m=TILES),
                        in_=sums_of[:, part * P // parts : (part + 1) * P // parts],
                    )
                    nc.sync.dma_start(
                        out=out_dram[j][:, part * channels : (part + 1) * channels], in_=result[:]
                    )
            summed.clear()

        turned = []
        waiting = []
        x_passes_done = [0] * IMAGES
        begun = 0

        def finish_oldest():
            operand, n, j, first, count, grouped = turned[0][1:]
            turned.remove(turned[0])
            if operand == "x":
                finish_x(n, j, first, count, grouped)
                x_passes_done[n] += count
            else:
                finish_dy(n, j, first, count, grouped)
                waiting.append((n, j, first, count))
            if waiting and x_passes_done[waiting[0][0]] == PASSES * TILES // PAIR:
                multiply(*waiting[0])
                waiting.remove(waiting[0])

        regular = len(steps) - len(taper)
        for i, (operand, n, j, first, count) in enumerate(steps):
            if operand == "dy":
                cols = tokens_of(first, count)
                if (n, j) != dy_tiles[-1]:
                    mask = work.tile([P, count * K_PASS], BF16, name="mask")
                    nc.vector.tensor_scalar(
                        out=mask[:],
                        in0=z_raw[(n, j)][:, cols],
                        scalar1=0.0,
                        scalar2=None,
                        op0=ALU.is_gt,
                    )
                if (n, j, first) not in scaled_of:
                    scale_g(n, j, first, count)
            for ahead in (1, 2):
                if i + ahead < len(steps) and steps[i + ahead][0] == "dy":
                    if steps[i + ahead][1:4] not in scaled_of and (ahead == 1 or on_scalar(*steps[i + ahead][1:4])):
                        scale_g(*steps[i + ahead][1:])
            if i < len(steps) - 1 and turned and begun - turned[0][0] >= LAG:
                finish_oldest()
            if operand == "dy":
                dy = work.tile([P, count * K_PASS], BF16, name="dy")
                if (n, j) != dy_tiles[-1]:
                    nc.vector.tensor_mul(out=dy[:], in0=scaled_of[(n, j, first)][:], in1=mask[:])
                else:
                    nc.vector.scalar_tensor_tensor(
                        out=dy[:],
                        in0=z_raw[(n, j)][:, cols],
                        scalar=0.0,
                        in1=scaled_of[(n, j, first)][:],
                        op0=ALU.is_gt,
                        op1=ALU.mult,
                    )
                grouped = lagged.tile([P, count * K_PASS], BF16, name="grouped", align_bytes=64)
                turn(
                    dy[:].bitcast(F32),
                    grouped[:].bitcast(F32).rearrange("p (g c u) -> p g c u", g=count, u=2),
                )
            else:
                if j % PAIR == 0:
                    x_grouped = lagged.tile(
                        [P, count * PAIR * K_PASS], BF16, name="x_grouped", align_bytes=64
                    )
                turn(
                    x_raw[(n, j - j % PAIR)][:, j % PAIR, tokens_of(first, count)].bitcast(F32),
                    x_grouped[:]
                    .bitcast(F32)
                    .rearrange("p (g m c u) -> p m g c u", g=count, m=PAIR, u=2)[:, j % PAIR],
                )
            if i < regular or i == len(steps) - 1:
                store_summed()
            begun += WORK[operand]
            if operand == "dy":
                turned.append((begun, operand, n, j, first, count, grouped))
            elif j % PAIR == PAIR - 1:
                turned.append((begun, operand, n, j - PAIR + 1, first, count, x_grouped))
        while turned:
            finish_oldest()
            store_summed()
